import numpy as np
import ml_dtypes


BF16 = ml_dtypes.bfloat16


def bf(x):
    return np.asarray(x, np.float32).astype(BF16)


def f64(x):
    return np.asarray(x).astype(np.float64)


E2M1 = np.array([0.0, 0.5, 1.0, 1.5, 2.0, 3.0, 4.0, 6.0, -0.0, -0.5, -1.0, -1.5, -2.0, -3.0, -4.0, -6.0])


def pack_weight(w, fmt):
    k, n = w.shape
    w = f64(bf(w)).reshape(k // 32, 32, n)
    amax = np.abs(w).max(1)
    if fmt == "e4m3":
        byte = np.frexp(amax)[1] - 1 + 127 - 7
    else:
        mant, ex = np.frexp(amax / 6.0)
        byte = np.where(mant > 0.5, ex, ex - 1) + 127
    byte = np.clip(np.where(amax > 0, byte, 1), 1, 254)
    scaled = (w * np.exp2(127.0 - byte)[:, None, :]).reshape(k, n).astype(np.float32)
    by_word = np.ascontiguousarray(scaled.reshape(k // 512, 128, 4, n).transpose(0, 1, 3, 2))
    if fmt == "e4m3":
        words = by_word.astype(ml_dtypes.float8_e4m3fn).view(np.uint8)
    else:
        c = by_word.astype(ml_dtypes.float4_e2m1fn).view(np.uint8) & 0xF
        words = c[..., 0::2] | (c[..., 1::2] << 4)
    return np.ascontiguousarray(words), np.ascontiguousarray(byte.astype(np.uint8).reshape(k // 512, 16, n))


def unpack_weight(words, scales, fmt):
    g, p, n, _ = words.shape
    if fmt == "e4m3":
        vals = np.ascontiguousarray(words).view(ml_dtypes.float8_e4m3fn).astype(np.float64)
    else:
        nib = np.empty((g, p, n, 4), np.uint8)
        nib[..., 0::2] = words & 0xF
        nib[..., 1::2] = words >> 4
        vals = E2M1[nib]
    vals = vals * np.repeat(np.exp2(scales.astype(np.float64) - 127.0), 8, axis=1)[..., None]
    return vals.transpose(0, 1, 3, 2).reshape(g * 512, n)

def pack4(w):
    words, scales = pack_weight(w, "e2m1")
    return words.reshape(words.shape[0], 128, -1), scales


def unpack4(words, scales):
    return unpack_weight(words.reshape(words.shape[0], 128, -1, 2), scales, "e2m1")


def kspread(k):
    return np.exp2(np.repeat(np.random.randint(-6, 7, k // 32), 32).astype(np.float64))


B, L, C, H, DH, AX = 2, 1024, 4096, 16, 192, 3
D3 = DH // AX
HALF = D3 // 2
ROPE_BASE = 10000.0
COORD_MAX = 10.0


def rope_3d(x, coords):
    inv_freq = 1.0 / (ROPE_BASE ** (np.arange(HALF) / HALF))
    ang = coords[..., None] * inv_freq
    cos = np.cos(ang)[:, None]
    sin = np.sin(ang)[:, None]
    xr = x.reshape(B, H, L, AX, D3)
    x1, x2 = xr[..., :HALF], xr[..., HALF:]
    out = np.concatenate([x1 * cos - x2 * sin, x1 * sin + x2 * cos], axis=-1)
    return out.reshape(B, H, L, DH)


def setup_inputs():
    s = kspread(C)
    x_in = np.random.standard_normal((B, L, C)) * s
    x_in_words, x_in_scales = pack4(np.ascontiguousarray(x_in.reshape(B * L, C).T))
    coords = bf(np.random.uniform(size=(B, L, AX)) * COORD_MAX)
    w = np.random.standard_normal((H * DH, C)) * 1.5 / np.sqrt(C) / s
    words, scales = pack4(np.ascontiguousarray(w.T))
    return {"x_in_words": x_in_words,
            "x_in_scales": x_in_scales,
            "coords": coords,
            "w_words": words,
            "w_scales": scales}


def reference(x_in_words, x_in_scales, coords, w_words, w_scales):
    x_in = unpack4(x_in_words, x_in_scales).T.reshape(B, L, C)
    p = x_in @ unpack4(w_words, w_scales)
    p = p.reshape(B, L, H, DH).transpose(0, 2, 1, 3)
    return rope_3d(p, f64(coords))

@@ -1,0 +1,342 @@
+import math
+from contextlib import ExitStack
+
+import concourse.mybir as mybir
+
+F32 = mybir.dt.float32
+BF16 = mybir.dt.bfloat16
+I32 = mybir.dt.int32
+U8 = mybir.dt.uint8
+FP4X4 = mybir.dt.float4_e2m1fn_x4
+ALU = mybir.AluOpType
+ACT = mybir.ActivationFunctionType
+
+P = 128
+B, L, C, H, DH, AX = 2, 1024, 4096, 16, 192, 3
+TOKENS = B * L
+FEATURES = H * DH
+PASSES = C // 512
+D3 = DH // AX
+HALF = D3 // 2
+N_TILE = 512
+BANKS = 8
+GROUPS = 2
+GH = H // GROUPS
+GF = GH * DH
+TILES = TOKENS // P
+TILES_PER_B = L // P
+
+TOKEN_RANGES = ((0, 2), (2, 8), (8, 16))
+TABLE_RANGES = ((0, 2), (2, 6), (6, 11), (11, 16))
+
+TABLES_LATER = 6
+TABLES_LEAD = 4
+
+LOG_BASE = math.log(10000.0)
+TWO_PI_HI = 6.28125
+TWO_PI_LO = 2.0 * math.pi - TWO_PI_HI
+PI_F32 = 3.1415927410125732
+
+LAST_CHUNKS = ((512, (0, 2)), (256, (2, 4)), (256, (4, 5)), (256, (5, 6)), (128, (6, 7)), (128, (7, 8)))
+BY_CHUNK = 3
+GPSIMD_CHUNKS = 3
+WRAP = 8
+
+WARM_MATMULS = 8
+
+FLOPS = 2 * TOKENS * C * FEATURES
+
+
+def tile_crossattnrope_pa_kernel(tc, x_words, x_scales, coords, w_words, w_scales, out):
+    nc = tc.nc
+
+    with ExitStack() as ctx:
+        keep = ctx.enter_context(tc.tile_pool(name="keep", bufs=1))
+        turns_pool = ctx.enter_context(tc.tile_pool(name="turns", bufs=2))
+        work = ctx.enter_context(tc.tile_pool(name="work", bufs=3))
+        psum = ctx.enter_context(tc.psum_pool(name="psum", bufs=1))
+        ctx.enter_context(tc.manual_schedule())
+
+        x_codes, x_planes = [], []
+        for r, (first, end) in enumerate(TOKEN_RANGES):
+            cols = (end - first) * P
+            x_codes.append(keep.tile([P, PASSES, 2 * cols], U8, name="x_codes%d" % r, align_bytes=256))
+            x_planes.append(keep.tile([P, PASSES, cols], U8, name="x_planes%d" % r, align_bytes=256))
+        w_codes, w_planes = [], []
+        for grp in range(GROUPS):
+            w_codes.append(keep.tile([P, PASSES, 2 * GF], U8, name="w_codes%d" % grp, align_bytes=256))
+            w_planes.append(keep.tile([P, PASSES, GF], U8, name="w_planes%d" % grp, align_bytes=256))
+
+        cos_tab = keep.tile([P, TILES, DH], F32, name="cos_tab")
+        sin_tab = keep.tile([P, TILES, DH], F32, name="sin_tab")
+
+        def load_x_codes(r, g0, g1):
+            first, end = TOKEN_RANGES[r]
+            nc.sync.dma_start(
+                out=x_codes[r][:, g0:g1, :].bitcast(I32),
+                in_=x_words[g0:g1, :, 2 * P * first : 2 * P * end].rearrange("g p n -> p g n").bitcast(I32),
+            )
+
+        def load_w_codes(grp, g, c0, c1):
+            nc.sync.dma_start(
+                out=w_codes[grp][:, g, 2 * c0 : 2 * c1].bitcast(I32),
+                in_=w_words[g, :, 2 * (GF * grp + c0) : 2 * (GF * grp + c1)].bitcast(I32),
+            )
+
+        def load_planes(plane, scales, g0, g1, c0, c1):
+            for q in (0, 2, 1, 3):
+                nc.sync.dma_start(
+                    out=plane[32 * q : 32 * q + 4, g0:g1, :].bitcast(I32),
+                    in_=scales[g0:g1, 4 * q : 4 * q + 4, c0:c1].rearrange("g r n -> r g n").bitcast(I32),
+                )
+
+        def load_x_planes(r):
+            first, end = TOKEN_RANGES[r]
+            load_planes(x_planes[r], x_scales, 0, PASSES, P * first, P * end)
+
+        def load_w_planes(grp, g0, g1):
+            load_planes(w_planes[grp], w_scales, g0, g1, GF * grp, GF * (grp + 1))
+
+        nc.vector.memset(x_planes[0][:].bitcast(I32), 0)
+        nc.vector.memset(w_planes[0][:, 0:2, :].bitcast(I32), 0)
+        nc.vector.memset(w_planes[0][:, 2:PASSES, :].bitcast(I32), 0)
+
+        zeros = keep.tile([P, N_TILE], BF16, name="zeros")
+        nc.gpsimd.memset(zeros[:], 0.0)
+        coord_sb = keep.tile([P, TILES, 4], BF16, name="coord_sb")
+        nc.gpsimd.dma_start(
+            out=coord_sb[:, :, 0:AX],
+            in_=coords.rearrange("b l a -> (b l) a").rearrange("(t p) a -> p t a", p=P),
+        )
+        inv_freq = keep.tile([P, HALF], F32, name="inv_freq")
+        nc.gpsimd.memset(inv_freq[:, 0:1], 1.0)
+        known = 1
+        while known < HALF:
+            nc.gpsimd.tensor_scalar(
+                out=inv_freq[:, known : 2 * known],
+                in0=inv_freq[:, 0:known],
+                scalar1=math.exp(-LOG_BASE * known / HALF),
+                scalar2=0.0,
+                op0=ALU.mult,
+                op1=ALU.add,
+            )
+            known *= 2
+        nc.gpsimd.memset(x_planes[1][:].bitcast(I32), 0)
+        nc.gpsimd.memset(x_planes[2][:].bitcast(I32), 0)
+        nc.gpsimd.memset(w_planes[1][:].bitcast(I32), 0)
+
+        first_sin = keep.tile([P, 1], F32, name="first_sin")
+        nc.scalar.activation(out=first_sin[:], in_=zeros[:, 0:1], func=ACT.Sin)
+
+        load_x_codes(0, 0, 1)
+        load_w_codes(0, 0, 0, N_TILE)
+        load_x_planes(0)
+        load_w_planes(0, 0, 2)
+        load_w_codes(0, 0, N_TILE, GF)
+        load_w_codes(0, 1, 0, GF)
+        load_x_codes(0, 1, PASSES)
+        load_w_planes(0, 2, PASSES)
+        for g in range(2, PASSES):
+            load_w_codes(0, g, 0, GF)
+        load_x_planes(1)
+        load_x_codes(1, 0, 4)
+        load_x_codes(1, 4, PASSES)
+
+        def make_angles(first, end):
+            n = end - first
+            ang = keep.tile([P, 2, n * AX * HALF], F32, name="ang%d" % first)
+            turns = turns_pool.tile([P, 2, n * AX * HALF], I32, name="turns")
+            nc.vector.tensor_tensor(
+                out=ang[:, 0, :].rearrange("p (t a i) -> p t a i", t=n, a=AX),
+                in0=coord_sb[:, first:end, 0:AX].unsqueeze(3).to_broadcast([P, n, AX, HALF]),
+                in1=inv_freq[:].unsqueeze(1).unsqueeze(1).to_broadcast([P, n, AX, HALF]),
+                op=ALU.mult,
+            )
+            nc.vector.tensor_scalar(
+                out=ang[:, 1, :], in0=ang[:, 0, :], scalar1=0.5 * math.pi, scalar2=None, op0=ALU.add
+            )
+            nc.vector.tensor_scalar(
+                out=turns[:], in0=ang[:], scalar1=0.5 / math.pi, scalar2=None, op0=ALU.mult
+            )
+            for part in (TWO_PI_HI, TWO_PI_LO):
+                nc.vector.scalar_tensor_tensor(
+                    out=ang[:], in0=turns[:], scalar=-part, in1=ang[:], op0=ALU.mult, op1=ALU.add
+                )
+            nc.vector.tensor_scalar(
+                out=ang[:], in0=ang[:], scalar1=PI_F32, scalar2=-PI_F32, op0=ALU.min, op1=ALU.max
+            )
+            return ang
+
+        def make_tables(ang, first, end):
+            pairs = (end - first) * AX
+            nc.scalar.activation(
+                out=cos_tab[:, first:end, :].rearrange("p t (a s i) -> p (t a) s i", a=AX, s=2),
+                in_=ang[:, 1, :].rearrange("p (m i) -> p m i", m=pairs).unsqueeze(2).to_broadcast([P, pairs, 2, HALF]),
+                func=ACT.Sin,
+            )
+            sin_view = sin_tab[:, first:end, :].rearrange("p t (a s i) -> p (t a) s i", a=AX, s=2)
+            for s, sign in ((0, -1.0), (1, 1.0)):
+                nc.scalar.activation(
+                    out=sin_view[:, :, s, :],
+                    in_=ang[:, 0, :].rearrange("p (m i) -> p m i", m=pairs),
+                    func=ACT.Sin,
+                    scale=sign,
+                )
+
+        later_tables = {}
+        for first, end in TABLE_RANGES:
+            ang = make_angles(first, end)
+            if first < TABLES_LATER:
+                make_tables(ang, first, end)
+            else:
+                later_tables[first - TABLES_LEAD] = (ang, first, end)
+
+        last_cos = keep.tile([P, WRAP * D3], F32, name="last_cos")
+        last_sin = keep.tile([P, WRAP * D3], F32, name="last_sin")
+
+        def make_wrapped_tables():
+            for wrapped, table in ((last_cos, cos_tab), (last_sin, sin_tab)):
+                for c0 in range(0, WRAP * D3, DH):
+                    n = min(DH, WRAP * D3 - c0)
+                    nc.gpsimd.tensor_copy(out=wrapped[:, c0 : c0 + n], in_=table[:, TILES - 1, 0:n])
+
+        next_bank = [0]
+
+        def new_bank():
+            bank = psum.tile([P, N_TILE], F32, name="bank%d" % next_bank[0])
+            next_bank[0] = (next_bank[0] + 1) % BANKS
+            return bank
+
+        def mm(bank, n, t, grp, c0, g):
+            r = 0
+            while t >= TOKEN_RANGES[r][1]:
+                r += 1
+            m0 = P * (t - TOKEN_RANGES[r][0])
+            nc.tensor.matmul_mx(
+                out=bank[:, 0:n],
+                lhsT=x_codes[r][:, g, 2 * m0 : 2 * (m0 + P)].bitcast(FP4X4),
+                lhsT_scale=x_planes[r][:, g, m0 : m0 + P],
+                rhs=w_codes[grp][:, g, 2 * c0 : 2 * (c0 + n)].bitcast(FP4X4),
+                rhs_scale=w_planes[grp][:, g, c0 : c0 + n],
+                start=(g == 0),
+                stop=(g == PASSES - 1),
+            )
+
+        def heads(tile, h0, h1):
+            return tile[:, DH * h0 : DH * h1].rearrange("p (h d) -> p h d", d=DH)
+
+        def times_cos(proj, rot, t, h0, h1):
+            nc.vector.tensor_tensor(
+                out=heads(rot, h0, h1),
+                in0=heads(proj, h0, h1),
+                in1=cos_tab[:, t, :].unsqueeze(1).to_broadcast([P, h1 - h0, DH]),
+                op=ALU.mult,
+            )
+
+        def times_sin(proj, cross, t, h0, h1):
+            src = heads(proj, h0, h1).rearrange("p h (a s i) -> p h a s i", a=AX, s=2)
+            dst = heads(cross, h0, h1).rearrange("p h (a s i) -> p h a s i", a=AX, s=2)
+            sin = sin_tab[:, t, :].rearrange("p (a s i) -> p a s i", a=AX, s=2)
+            for s in (0, 1):
+                nc.vector.tensor_tensor(
+                    out=dst[:, :, :, s, :],
+                    in0=src[:, :, :, 1 - s, :],
+                    in1=sin[:, :, s, :].unsqueeze(1).to_broadcast([P, h1 - h0, AX, HALF]),
+                    op=ALU.mult,
+                )
+
+        def store(rot, t, grp, h0, h1):
+            b, l0 = t // TILES_PER_B, P * (t % TILES_PER_B)
+            nc.sync.dma_start(
+                out=out[b, GH * grp + h0 : GH * grp + h1, l0 : l0 + P, :].rearrange("h l d -> l h d"),
+                in_=heads(rot, h0, h1),
+            )
+
+        def add_and_store(rot, cross, t, grp, h0, h1, adder=nc.vector):
+            cols = slice(DH * h0, DH * h1)
+            adder.tensor_tensor(out=rot[:, cols], in0=rot[:, cols], in1=cross[:, cols], op=ALU.add)
+            store(rot, t, grp, h0, h1)
+
+        later_loads = {
+            0: [lambda: load_x_planes(2), lambda: load_x_codes(2, 0, 4), lambda: load_x_codes(2, 4, PASSES)],
+            2: [lambda: load_w_planes(1, 0, PASSES)],
+        }
+        for i in range(4):
+            later_loads[3 + i] = [
+                lambda g=2 * i: load_w_codes(1, g, 0, GF),
+                lambda g=2 * i + 1: load_w_codes(1, g, 0, GF),
+            ]
+
+        units = [(t, grp) for grp in range(GROUPS) for t in range(TILES)]
+        last = len(units) - 1
+        chunks = [(c0, N_TILE) for c0 in range(0, GF, N_TILE)]
+
+        warm = psum.tile([P, N_TILE], F32, name="bank%d" % (BANKS - 1))
+        for i in range(WARM_MATMULS):
+            nc.tensor.matmul(out=warm[:], lhsT=zeros[:, 0:P], rhs=zeros[:], start=True, stop=True)
+
+        shared = (0, 1)
+        shared_banks = {(u, c0): new_bank() for u in shared for c0, n in chunks}
+        for g in range(PASSES):
+            if g < PASSES - 1:
+                order = [(u, c0) for c0, n in chunks for u in shared]
+            else:
+                order = [(u, c0) for u in shared for c0, n in chunks]
+            for u, c0 in order:
+                mm(shared_banks[u, c0], N_TILE, units[u][0], units[u][1], c0, g)
+
+        whole = ((N_TILE, None), (N_TILE, None), (N_TILE, (0, GH)))
+        by_chunk = ((N_TILE, (0, 2)), (N_TILE, (2, 5)), (N_TILE, (5, GH)))
+
+        pending = None
+        for u, (t, grp) in enumerate(units[:last]):
+            proj = work.tile([P, GF], F32, name="proj")
+            cross = work.tile([P, GF], F32, name="cross")
+            rot = work.tile([P, GF], F32, name="rot")
+            c0 = 0
+            for n, span in by_chunk if u >= last - BY_CHUNK else whole:
+                if u in shared:
+                    bank = shared_banks[u, c0]
+                else:
+                    bank = new_bank()
+                    for g in range(PASSES):
+                        mm(bank, n, t, grp, c0, g)
+                nc.scalar.copy(out=proj[:, c0 : c0 + n], in_=bank[:, 0:n])
+                c0 += n
+                if span is None:
+                    continue
+                h0, h1 = span
+                times_cos(proj, rot, t, h0, h1)
+                if pending is not None:
+                    add_and_store(*pending)
+                times_sin(proj, cross, t, h0, h1)
+                pending = (rot, cross, t, grp, h0, h1)
+            if u in later_tables:
+                make_tables(*later_tables[u])
+            if u == TILES:
+                make_wrapped_tables()
+            for load in later_loads.get(u - 1, ()):
+                load()
+        add_and_store(*pending, adder=nc.gpsimd)
+
+        t, grp = units[last]
+        cross = work.tile([P, GF], F32, name="cross")
+        rot = work.tile([P, GF], F32, name="rot")
+        c0 = 0
+        for i, (n, (h0, h1)) in enumerate(LAST_CHUNKS):
+            bank = new_bank()
+            for g in range(PASSES):
+                mm(bank, n, t, grp, c0, g)
+            cols = slice(c0, c0 + n)
+            axis = c0 // D3 % AX
+            table = slice(D3 * axis, D3 * axis + n)
+            nc.vector.tensor_tensor(out=rot[:, cols], in0=bank[:, 0:n], in1=last_cos[:, table], op=ALU.mult)
+            src = bank[:, 0:n].rearrange("p (m s i) -> p m s i", s=2, i=HALF)
+            dst = cross[:, cols].rearrange("p (m s i) -> p m s i", s=2, i=HALF)
+            sin = last_sin[:, table].rearrange("p (m s i) -> p m s i", s=2, i=HALF)
+            for s in (0, 1):
+                nc.vector.tensor_tensor(out=dst[:, :, s, :], in0=src[:, :, 1 - s, :], in1=sin[:, :, s, :], op=ALU.mult)
+            adder = nc.gpsimd if i < GPSIMD_CHUNKS else nc.vector
+            adder.tensor_tensor(out=rot[:, cols], in0=rot[:, cols], in1=cross[:, cols], op=ALU.add)
+            store(rot, t, grp, h0, h1)
+            c0 += n

@@ -26,7 +26,11 @@ GF = GH * DH
 TILES = TOKENS // P
 TILES_PER_B = L // P
 
-TOKEN_RANGES = ((0, 2), (2, 8), (8, 16))
+TOKEN_RANGES = ((0, 4), (4, 8), (8, 16))
+FEATURE_RANGES = ((0, 1024), (1024, 1536), (1536, 3072))
+SWEEP_TILES = TOKEN_RANGES[0][1]
+SWEEP_CHUNKS = FEATURE_RANGES[0][1] // N_TILE
+SWEEP_HEADS = 5
 TABLE_RANGES = ((0, 2), (2, 6), (6, 11), (11, 16))
 
 TABLES_LATER = 6
@@ -38,6 +42,7 @@ TWO_PI_LO = 2.0 * math.pi - TWO_PI_HI
 PI_F32 = 3.1415927410125732
 
 LAST_CHUNKS = ((512, (0, 2)), (256, (2, 4)), (256, (4, 5)), (256, (5, 6)), (128, (6, 7)), (128, (7, 8)))
+PROJ_BUFS = 5
 BY_CHUNK = 3
 GPSIMD_CHUNKS = 3
 WRAP = 8
@@ -53,7 +58,7 @@ def tile_crossattnrope_pa_kernel(tc, x_words, x_scales, coords, w_words, w_scale
     with ExitStack() as ctx:
         keep = ctx.enter_context(tc.tile_pool(name="keep", bufs=1))
         turns_pool = ctx.enter_context(tc.tile_pool(name="turns", bufs=2))
-        work = ctx.enter_context(tc.tile_pool(name="work", bufs=3))
+        work = ctx.enter_context(tc.tile_pool(name="work", bufs=1))
         psum = ctx.enter_context(tc.psum_pool(name="psum", bufs=1))
         ctx.enter_context(tc.manual_schedule())
 
@@ -63,9 +68,10 @@ def tile_crossattnrope_pa_kernel(tc, x_words, x_scales, coords, w_words, w_scale
             x_codes.append(keep.tile([P, PASSES, 2 * cols], U8, name="x_codes%d" % r, align_bytes=256))
             x_planes.append(keep.tile([P, PASSES, cols], U8, name="x_planes%d" % r, align_bytes=256))
         w_codes, w_planes = [], []
-        for grp in range(GROUPS):
-            w_codes.append(keep.tile([P, PASSES, 2 * GF], U8, name="w_codes%d" % grp, align_bytes=256))
-            w_planes.append(keep.tile([P, PASSES, GF], U8, name="w_planes%d" % grp, align_bytes=256))
+        for r, (first, end) in enumerate(FEATURE_RANGES):
+            cols = end - first
+            w_codes.append(keep.tile([P, PASSES, 2 * cols], U8, name="w_codes%d" % r, align_bytes=256))
+            w_planes.append(keep.tile([P, PASSES, cols], U8, name="w_planes%d" % r, align_bytes=256))
 
         cos_tab = keep.tile([P, TILES, DH], F32, name="cos_tab")
         sin_tab = keep.tile([P, TILES, DH], F32, name="sin_tab")
@@ -77,10 +83,18 @@ def tile_crossattnrope_pa_kernel(tc, x_words, x_scales, coords, w_words, w_scale
                 in_=x_words[g0:g1, :, 2 * P * first : 2 * P * end].rearrange("g p n -> p g n").bitcast(I32),
             )
 
-        def load_w_codes(grp, g, c0, c1):
+        def load_w_columns(r, g, c0, c1):
+            first = FEATURE_RANGES[r][0]
             nc.sync.dma_start(
-                out=w_codes[grp][:, g, 2 * c0 : 2 * c1].bitcast(I32),
-                in_=w_words[g, :, 2 * (GF * grp + c0) : 2 * (GF * grp + c1)].bitcast(I32),
+                out=w_codes[r][:, g, 2 * c0 : 2 * c1].bitcast(I32),
+                in_=w_words[g, :, 2 * (first + c0) : 2 * (first + c1)].bitcast(I32),
+            )
+
+        def load_w_codes(r, g0, g1):
+            first, end = FEATURE_RANGES[r]
+            nc.sync.dma_start(
+                out=w_codes[r][:, g0:g1, :].bitcast(I32),
+                in_=w_words[g0:g1, :, 2 * first : 2 * end].rearrange("g p n -> p g n").bitcast(I32),
             )
 
         def load_planes(plane, scales, g0, g1, c0, c1):
@@ -94,11 +108,12 @@ def tile_crossattnrope_pa_kernel(tc, x_words, x_scales, coords, w_words, w_scale
             first, end = TOKEN_RANGES[r]
             load_planes(x_planes[r], x_scales, 0, PASSES, P * first, P * end)
 
-        def load_w_planes(grp, g0, g1):
-            load_planes(w_planes[grp], w_scales, g0, g1, GF * grp, GF * (grp + 1))
+        def load_w_planes(r, g0, g1):
+            first, end = FEATURE_RANGES[r]
+            load_planes(w_planes[r], w_scales, g0, g1, first, end)
 
         nc.vector.memset(x_planes[0][:].bitcast(I32), 0)
-        nc.vector.memset(w_planes[0][:, 0:2, :].bitcast(I32), 0)
+        nc.gpsimd.memset(w_planes[0][:, 0:2, :].bitcast(I32), 0)
         nc.vector.memset(w_planes[0][:, 2:PASSES, :].bitcast(I32), 0)
 
         zeros = keep.tile([P, N_TILE], BF16, name="zeros")
@@ -121,23 +136,29 @@ def tile_crossattnrope_pa_kernel(tc, x_words, x_scales, coords, w_words, w_scale
                 op1=ALU.add,
             )
             known *= 2
-        nc.gpsimd.memset(x_planes[1][:].bitcast(I32), 0)
-        nc.gpsimd.memset(x_planes[2][:].bitcast(I32), 0)
-        nc.gpsimd.memset(w_planes[1][:].bitcast(I32), 0)
+        for plane in (w_planes[1], x_planes[1], x_planes[2], w_planes[2]):
+            nc.gpsimd.memset(plane[:].bitcast(I32), 0)
 
         first_sin = keep.tile([P, 1], F32, name="first_sin")
         nc.scalar.activation(out=first_sin[:], in_=zeros[:, 0:1], func=ACT.Sin)
 
         load_x_codes(0, 0, 1)
-        load_w_codes(0, 0, 0, N_TILE)
+        load_w_columns(0, 0, 0, N_TILE)
         load_x_planes(0)
         load_w_planes(0, 0, 2)
-        load_w_codes(0, 0, N_TILE, GF)
-        load_w_codes(0, 1, 0, GF)
-        load_x_codes(0, 1, PASSES)
-        load_w_planes(0, 2, PASSES)
-        for g in range(2, PASSES):
-            load_w_codes(0, g, 0, GF)
+        load_w_columns(0, 0, N_TILE, FEATURE_RANGES[0][1])
+        load_w_codes(0, 1, 2)
+        load_x_codes(0, 1, 4)
+        load_w_planes(0, 2, 5)
+        for g in (2, 3, 4):
+            load_w_codes(0, g, g + 1)
+        load_x_codes(0, 4, PASSES)
+        load_w_planes(0, 5, PASSES)
+        for g in (5, 6, 7):
+            load_w_codes(0, g, g + 1)
+        load_w_planes(1, 0, PASSES)
+        load_w_codes(1, 0, 4)
+        load_w_codes(1, 4, PASSES)
         load_x_planes(1)
         load_x_codes(1, 0, 4)
         load_x_codes(1, 4, PASSES)
@@ -208,16 +229,17 @@ def tile_crossattnrope_pa_kernel(tc, x_words, x_scales, coords, w_words, w_scale
             return bank
 
         def mm(bank, n, t, grp, c0, g):
-            r = 0
-            while t >= TOKEN_RANGES[r][1]:
-                r += 1
+            r = [t < end for first, end in TOKEN_RANGES].index(True)
             m0 = P * (t - TOKEN_RANGES[r][0])
+            f0 = GF * grp + c0
+            s = [f0 < end for first, end in FEATURE_RANGES].index(True)
+            f0 -= FEATURE_RANGES[s][0]
             nc.tensor.matmul_mx(
                 out=bank[:, 0:n],
                 lhsT=x_codes[r][:, g, 2 * m0 : 2 * (m0 + P)].bitcast(FP4X4),
                 lhsT_scale=x_planes[r][:, g, m0 : m0 + P],
-                rhs=w_codes[grp][:, g, 2 * c0 : 2 * (c0 + n)].bitcast(FP4X4),
-                rhs_scale=w_planes[grp][:, g, c0 : c0 + n],
+                rhs=w_codes[s][:, g, 2 * f0 : 2 * (f0 + n)].bitcast(FP4X4),
+                rhs_scale=w_planes[s][:, g, f0 : f0 + n],
                 start=(g == 0),
                 stop=(g == PASSES - 1),
             )
@@ -257,51 +279,56 @@ def tile_crossattnrope_pa_kernel(tc, x_words, x_scales, coords, w_words, w_scale
             adder.tensor_tensor(out=rot[:, cols], in0=rot[:, cols], in1=cross[:, cols], op=ALU.add)
             store(rot, t, grp, h0, h1)
 
-        later_loads = {
-            0: [lambda: load_x_planes(2), lambda: load_x_codes(2, 0, 4), lambda: load_x_codes(2, 4, PASSES)],
-            2: [lambda: load_w_planes(1, 0, PASSES)],
-        }
-        for i in range(4):
-            later_loads[3 + i] = [
-                lambda g=2 * i: load_w_codes(1, g, 0, GF),
-                lambda g=2 * i + 1: load_w_codes(1, g, 0, GF),
-            ]
+        def later_loads(u):
+            if u == 0:
+                load_x_planes(2)
+                load_x_codes(2, 0, 4)
+                load_x_codes(2, 4, PASSES)
+            elif u == 2:
+                load_w_planes(2, 0, PASSES)
+            elif 3 <= u < 7:
+                load_w_codes(2, 2 * (u - 3), 2 * (u - 2))
 
         units = [(t, grp) for grp in range(GROUPS) for t in range(TILES)]
         last = len(units) - 1
-        chunks = [(c0, N_TILE) for c0 in range(0, GF, N_TILE)]
 
         warm = psum.tile([P, N_TILE], F32, name="bank%d" % (BANKS - 1))
         for i in range(WARM_MATMULS):
             nc.tensor.matmul(out=warm[:], lhsT=zeros[:, 0:P], rhs=zeros[:], start=True, stop=True)
 
-        shared = (0, 1)
-        shared_banks = {(u, c0): new_bank() for u in shared for c0, n in chunks}
+        sweep = [(t, c) for t in range(SWEEP_TILES) for c in range(SWEEP_CHUNKS)]
+        sweep_banks = {key: new_bank() for key in sweep}
+        by_column = [(t, c) for c in range(SWEEP_CHUNKS) for t in range(SWEEP_TILES)]
         for g in range(PASSES):
-            if g < PASSES - 1:
-                order = [(u, c0) for c0, n in chunks for u in shared]
-            else:
-                order = [(u, c0) for u in shared for c0, n in chunks]
-            for u, c0 in order:
-                mm(shared_banks[u, c0], N_TILE, units[u][0], units[u][1], c0, g)
+            for t, c in by_column if g < PASSES - 1 else sweep:
+                mm(sweep_banks[t, c], N_TILE, t, 0, N_TILE * c, g)
+        sweep_proj = []
+        for t in range(SWEEP_TILES):
+            proj = work.tile([P, GF], F32, name="proj", bufs=PROJ_BUFS)
+            for c in range(SWEEP_CHUNKS):
+                nc.scalar.copy(out=proj[:, N_TILE * c : N_TILE * (c + 1)], in_=sweep_banks[t, c][:])
+            sweep_proj.append(proj)
 
         whole = ((N_TILE, None), (N_TILE, None), (N_TILE, (0, GH)))
         by_chunk = ((N_TILE, (0, 2)), (N_TILE, (2, 5)), (N_TILE, (5, GH)))
+        swept = ((N_TILE * SWEEP_CHUNKS, (0, SWEEP_HEADS)), (N_TILE, (SWEEP_HEADS, GH)))
 
         pending = None
         for u, (t, grp) in enumerate(units[:last]):
-            proj = work.tile([P, GF], F32, name="proj")
-            cross = work.tile([P, GF], F32, name="cross")
-            rot = work.tile([P, GF], F32, name="rot")
+            if u < SWEEP_TILES:
+                proj, spans = sweep_proj[u], swept
+            else:
+                proj = work.tile([P, GF], F32, name="proj", bufs=PROJ_BUFS)
+                spans = by_chunk if u >= last - BY_CHUNK else whole
+            cross = work.tile([P, GF], F32, name="cross", bufs=2)
+            rot = work.tile([P, GF], F32, name="rot", bufs=3)
             c0 = 0
-            for n, span in by_chunk if u >= last - BY_CHUNK else whole:
-                if u in shared:
-                    bank = shared_banks[u, c0]
-                else:
+            for n, span in spans:
+                if u >= SWEEP_TILES or c0 > 0:
                     bank = new_bank()
                     for g in range(PASSES):
                         mm(bank, n, t, grp, c0, g)
-                nc.scalar.copy(out=proj[:, c0 : c0 + n], in_=bank[:, 0:n])
+                    nc.scalar.copy(out=proj[:, c0 : c0 + n], in_=bank[:])
                 c0 += n
                 if span is None:
                     continue
@@ -315,13 +342,12 @@ def tile_crossattnrope_pa_kernel(tc, x_words, x_scales, coords, w_words, w_scale
                 make_tables(*later_tables[u])
             if u == TILES:
                 make_wrapped_tables()
-            for load in later_loads.get(u - 1, ()):
-                load()
+            later_loads(u - 1)
         add_and_store(*pending, adder=nc.gpsimd)
 
         t, grp = units[last]
-        cross = work.tile([P, GF], F32, name="cross")
-        rot = work.tile([P, GF], F32, name="rot")
+        cross = work.tile([P, GF], F32, name="cross", bufs=2)
+        rot = work.tile([P, GF], F32, name="rot", bufs=3)
         c0 = 0
         for i, (n, (h0, h1)) in enumerate(LAST_CHUNKS):
             bank = new_bank()

@@ -41,11 +41,11 @@ TWO_PI_HI = 6.28125
 TWO_PI_LO = 2.0 * math.pi - TWO_PI_HI
 PI_F32 = 3.1415927410125732
 
-LAST_CHUNKS = ((512, (0, 2)), (256, (2, 4)), (256, (4, 5)), (256, (5, 6)), (128, (6, 7)), (128, (7, 8)))
+LAST_CHUNKS = ((512, (0, 2)), (512, (2, 5)), (256, (5, 6)), (128, (6, 7)), (128, (7, 8)))
 PROJ_BUFS = 5
 BY_CHUNK = 3
-GPSIMD_CHUNKS = 3
-WRAP = 8
+GPSIMD_CHUNKS = 2
+WRAP = 10
 
 WARM_MATMULS = 8
 
@@ -62,16 +62,20 @@ def tile_crossattnrope_pa_kernel(tc, x_words, x_scales, coords, w_words, w_scale
         psum = ctx.enter_context(tc.psum_pool(name="psum", bufs=1))
         ctx.enter_context(tc.manual_schedule())
 
+        def operand_tile(name, width, start):
+            tile = keep.tile([P, start + PASSES * width], U8, name=name, align_bytes=256)
+            return tile[:, start:].rearrange("p (g n) -> p g n", g=PASSES)
+
         x_codes, x_planes = [], []
         for r, (first, end) in enumerate(TOKEN_RANGES):
             cols = (end - first) * P
-            x_codes.append(keep.tile([P, PASSES, 2 * cols], U8, name="x_codes%d" % r, align_bytes=256))
-            x_planes.append(keep.tile([P, PASSES, cols], U8, name="x_planes%d" % r, align_bytes=256))
+            x_codes.append(operand_tile("x_codes%d" % r, 2 * cols, 64))
+            x_planes.append(operand_tile("x_planes%d" % r, cols, 192))
         w_codes, w_planes = [], []
         for r, (first, end) in enumerate(FEATURE_RANGES):
             cols = end - first
-            w_codes.append(keep.tile([P, PASSES, 2 * cols], U8, name="w_codes%d" % r, align_bytes=256))
-            w_planes.append(keep.tile([P, PASSES, cols], U8, name="w_planes%d" % r, align_bytes=256))
+            w_codes.append(operand_tile("w_codes%d" % r, 2 * cols, 0))
+            w_planes.append(operand_tile("w_planes%d" % r, cols, 128))
 
         cos_tab = keep.tile([P, TILES, DH], F32, name="cos_tab")
         sin_tab = keep.tile([P, TILES, DH], F32, name="sin_tab")

import math
from contextlib import ExitStack

import concourse.mybir as mybir

F32 = mybir.dt.float32
BF16 = mybir.dt.bfloat16
I32 = mybir.dt.int32
U8 = mybir.dt.uint8
FP4X4 = mybir.dt.float4_e2m1fn_x4
ALU = mybir.AluOpType
ACT = mybir.ActivationFunctionType

P = 128
B, L, C, H, DH, AX = 2, 1024, 4096, 16, 192, 3
TOKENS = B * L
FEATURES = H * DH
PASSES = C // 512
D3 = DH // AX
HALF = D3 // 2
N_TILE = 512
BANKS = 8
GROUPS = 2
GH = H // GROUPS
GF = GH * DH
TILES = TOKENS // P
TILES_PER_B = L // P

TOKEN_RANGES = ((0, 4), (4, 8), (8, 16))
FEATURE_RANGES = ((0, 1024), (1024, 1536), (1536, 3072))
SWEEP_TILES = TOKEN_RANGES[0][1]
SWEEP_CHUNKS = FEATURE_RANGES[0][1] // N_TILE
SWEEP_HEADS = 5
TABLE_RANGES = ((0, 2), (2, 6), (6, 11), (11, 16))

TABLES_LATER = 6
TABLES_LEAD = 4

LOG_BASE = math.log(10000.0)
TWO_PI_HI = 6.28125
TWO_PI_LO = 2.0 * math.pi - TWO_PI_HI
PI_F32 = 3.1415927410125732

LAST_CHUNKS = ((512, (0, 2)), (512, (2, 5)), (256, (5, 6)), (128, (6, 7)), (128, (7, 8)))
PROJ_BUFS = 5
BY_CHUNK = 3
GPSIMD_CHUNKS = 2
WRAP = 10

WARM_MATMULS = 8

FLOPS = 2 * TOKENS * C * FEATURES


def tile_crossattnrope_pa_kernel(tc, x_words, x_scales, coords, w_words, w_scales, out):
    nc = tc.nc

    with ExitStack() as ctx:
        keep = ctx.enter_context(tc.tile_pool(name="keep", bufs=1))
        turns_pool = ctx.enter_context(tc.tile_pool(name="turns", bufs=2))
        work = ctx.enter_context(tc.tile_pool(name="work", bufs=1))
        psum = ctx.enter_context(tc.psum_pool(name="psum", bufs=1))
        ctx.enter_context(tc.manual_schedule())

        def operand_tile(name, width, start):
            tile = keep.tile([P, start + PASSES * width], U8, name=name, align_bytes=256)
            return tile[:, start:].rearrange("p (g n) -> p g n", g=PASSES)

        x_codes, x_planes = [], []
        for r, (first, end) in enumerate(TOKEN_RANGES):
            cols = (end - first) * P
            x_codes.append(operand_tile("x_codes%d" % r, 2 * cols, 64))
            x_planes.append(operand_tile("x_planes%d" % r, cols, 192))
        w_codes, w_planes = [], []
        for r, (first, end) in enumerate(FEATURE_RANGES):
            cols = end - first
            w_codes.append(operand_tile("w_codes%d" % r, 2 * cols, 0))
            w_planes.append(operand_tile("w_planes%d" % r, cols, 128))

        cos_tab = keep.tile([P, TILES, DH], F32, name="cos_tab")
        sin_tab = keep.tile([P, TILES, DH], F32, name="sin_tab")

        def load_x_codes(r, g0, g1):
            first, end = TOKEN_RANGES[r]
            nc.sync.dma_start(
                out=x_codes[r][:, g0:g1, :].bitcast(I32),
                in_=x_words[g0:g1, :, 2 * P * first : 2 * P * end].rearrange("g p n -> p g n").bitcast(I32),
            )

        def load_w_columns(r, g, c0, c1):
            first = FEATURE_RANGES[r][0]
            nc.sync.dma_start(
                out=w_codes[r][:, g, 2 * c0 : 2 * c1].bitcast(I32),
                in_=w_words[g, :, 2 * (first + c0) : 2 * (first + c1)].bitcast(I32),
            )

        def load_w_codes(r, g0, g1):
            first, end = FEATURE_RANGES[r]
            nc.sync.dma_start(
                out=w_codes[r][:, g0:g1, :].bitcast(I32),
                in_=w_words[g0:g1, :, 2 * first : 2 * end].rearrange("g p n -> p g n").bitcast(I32),
            )

        def load_planes(plane, scales, g0, g1, c0, c1):
            for q in (0, 2, 1, 3):
                nc.sync.dma_start(
                    out=plane[32 * q : 32 * q + 4, g0:g1, :].bitcast(I32),
                    in_=scales[g0:g1, 4 * q : 4 * q + 4, c0:c1].rearrange("g r n -> r g n").bitcast(I32),
                )

        def load_x_planes(r):
            first, end = TOKEN_RANGES[r]
            load_planes(x_planes[r], x_scales, 0, PASSES, P * first, P * end)

        def load_w_planes(r, g0, g1):
            first, end = FEATURE_RANGES[r]
            load_planes(w_planes[r], w_scales, g0, g1, first, end)

        nc.vector.memset(x_planes[0][:].bitcast(I32), 0)
        nc.gpsimd.memset(w_planes[0][:, 0:2, :].bitcast(I32), 0)
        nc.vector.memset(w_planes[0][:, 2:PASSES, :].bitcast(I32), 0)

        zeros = keep.tile([P, N_TILE], BF16, name="zeros")
        nc.gpsimd.memset(zeros[:], 0.0)
        coord_sb = keep.tile([P, TILES, 4], BF16, name="coord_sb")
        nc.gpsimd.dma_start(
            out=coord_sb[:, :, 0:AX],
            in_=coords.rearrange("b l a -> (b l) a").rearrange("(t p) a -> p t a", p=P),
        )
        inv_freq = keep.tile([P, HALF], F32, name="inv_freq")
        nc.gpsimd.memset(inv_freq[:, 0:1], 1.0)
        known = 1
        while known < HALF:
            nc.gpsimd.tensor_scalar(
                out=inv_freq[:, known : 2 * known],
                in0=inv_freq[:, 0:known],
                scalar1=math.exp(-LOG_BASE * known / HALF),
                scalar2=0.0,
                op0=ALU.mult,
                op1=ALU.add,
            )
            known *= 2
        for plane in (w_planes[1], x_planes[1], x_planes[2], w_planes[2]):
            nc.gpsimd.memset(plane[:].bitcast(I32), 0)

        first_sin = keep.tile([P, 1], F32, name="first_sin")
        nc.scalar.activation(out=first_sin[:], in_=zeros[:, 0:1], func=ACT.Sin)

        load_x_codes(0, 0, 1)
        load_w_columns(0, 0, 0, N_TILE)
        load_x_planes(0)
        load_w_planes(0, 0, 2)
        load_w_columns(0, 0, N_TILE, FEATURE_RANGES[0][1])
        load_w_codes(0, 1, 2)
        load_x_codes(0, 1, 4)
        load_w_planes(0, 2, 5)
        for g in (2, 3, 4):
            load_w_codes(0, g, g + 1)
        load_x_codes(0, 4, PASSES)
        load_w_planes(0, 5, PASSES)
        for g in (5, 6, 7):
            load_w_codes(0, g, g + 1)
        load_w_planes(1, 0, PASSES)
        load_w_codes(1, 0, 4)
        load_w_codes(1, 4, PASSES)
        load_x_planes(1)
        load_x_codes(1, 0, 4)
        load_x_codes(1, 4, PASSES)

        def make_angles(first, end):
            n = end - first
            ang = keep.tile([P, 2, n * AX * HALF], F32, name="ang%d" % first)
            turns = turns_pool.tile([P, 2, n * AX * HALF], I32, name="turns")
            nc.vector.tensor_tensor(
                out=ang[:, 0, :].rearrange("p (t a i) -> p t a i", t=n, a=AX),
                in0=coord_sb[:, first:end, 0:AX].unsqueeze(3).to_broadcast([P, n, AX, HALF]),
                in1=inv_freq[:].unsqueeze(1).unsqueeze(1).to_broadcast([P, n, AX, HALF]),
                op=ALU.mult,
            )
            nc.vector.tensor_scalar(
                out=ang[:, 1, :], in0=ang[:, 0, :], scalar1=0.5 * math.pi, scalar2=None, op0=ALU.add
            )
            nc.vector.tensor_scalar(
                out=turns[:], in0=ang[:], scalar1=0.5 / math.pi, scalar2=None, op0=ALU.mult
            )
            for part in (TWO_PI_HI, TWO_PI_LO):
                nc.vector.scalar_tensor_tensor(
                    out=ang[:], in0=turns[:], scalar=-part, in1=ang[:], op0=ALU.mult, op1=ALU.add
                )
            nc.vector.tensor_scalar(
                out=ang[:], in0=ang[:], scalar1=PI_F32, scalar2=-PI_F32, op0=ALU.min, op1=ALU.max
            )
            return ang

        def make_tables(ang, first, end):
            pairs = (end - first) * AX
            nc.scalar.activation(
                out=cos_tab[:, first:end, :].rearrange("p t (a s i) -> p (t a) s i", a=AX, s=2),
                in_=ang[:, 1, :].rearrange("p (m i) -> p m i", m=pairs).unsqueeze(2).to_broadcast([P, pairs, 2, HALF]),
                func=ACT.Sin,
            )
            sin_view = sin_tab[:, first:end, :].rearrange("p t (a s i) -> p (t a) s i", a=AX, s=2)
            for s, sign in ((0, -1.0), (1, 1.0)):
                nc.scalar.activation(
                    out=sin_view[:, :, s, :],
                    in_=ang[:, 0, :].rearrange("p (m i) -> p m i", m=pairs),
                    func=ACT.Sin,
                    scale=sign,
                )

        later_tables = {}
        for first, end in TABLE_RANGES:
            ang = make_angles(first, end)
            if first < TABLES_LATER:
                make_tables(ang, first, end)
            else:
                later_tables[first - TABLES_LEAD] = (ang, first, end)

        last_cos = keep.tile([P, WRAP * D3], F32, name="last_cos")
        last_sin = keep.tile([P, WRAP * D3], F32, name="last_sin")

        def make_wrapped_tables():
            for wrapped, table in ((last_cos, cos_tab), (last_sin, sin_tab)):
                for c0 in range(0, WRAP * D3, DH):
                    n = min(DH, WRAP * D3 - c0)
                    nc.gpsimd.tensor_copy(out=wrapped[:, c0 : c0 + n], in_=table[:, TILES - 1, 0:n])

        next_bank = [0]

        def new_bank():
            bank = psum.tile([P, N_TILE], F32, name="bank%d" % next_bank[0])
            next_bank[0] = (next_bank[0] + 1) % BANKS
            return bank

        def mm(bank, n, t, grp, c0, g):
            r = [t < end for first, end in TOKEN_RANGES].index(True)
            m0 = P * (t - TOKEN_RANGES[r][0])
            f0 = GF * grp + c0
            s = [f0 < end for first, end in FEATURE_RANGES].index(True)
            f0 -= FEATURE_RANGES[s][0]
            nc.tensor.matmul_mx(
                out=bank[:, 0:n],
                lhsT=x_codes[r][:, g, 2 * m0 : 2 * (m0 + P)].bitcast(FP4X4),
                lhsT_scale=x_planes[r][:, g, m0 : m0 + P],
                rhs=w_codes[s][:, g, 2 * f0 : 2 * (f0 + n)].bitcast(FP4X4),
                rhs_scale=w_planes[s][:, g, f0 : f0 + n],
                start=(g == 0),
                stop=(g == PASSES - 1),
            )

        def heads(tile, h0, h1):
            return tile[:, DH * h0 : DH * h1].rearrange("p (h d) -> p h d", d=DH)

        def times_cos(proj, rot, t, h0, h1):
            nc.vector.tensor_tensor(
                out=heads(rot, h0, h1),
                in0=heads(proj, h0, h1),
                in1=cos_tab[:, t, :].unsqueeze(1).to_broadcast([P, h1 - h0, DH]),
                op=ALU.mult,
            )

        def times_sin(proj, cross, t, h0, h1):
            src = heads(proj, h0, h1).rearrange("p h (a s i) -> p h a s i", a=AX, s=2)
            dst = heads(cross, h0, h1).rearrange("p h (a s i) -> p h a s i", a=AX, s=2)
            sin = sin_tab[:, t, :].rearrange("p (a s i) -> p a s i", a=AX, s=2)
            for s in (0, 1):
                nc.vector.tensor_tensor(
                    out=dst[:, :, :, s, :],
                    in0=src[:, :, :, 1 - s, :],
                    in1=sin[:, :, s, :].unsqueeze(1).to_broadcast([P, h1 - h0, AX, HALF]),
                    op=ALU.mult,
                )

        def store(rot, t, grp, h0, h1):
            b, l0 = t // TILES_PER_B, P * (t % TILES_PER_B)
            nc.sync.dma_start(
                out=out[b, GH * grp + h0 : GH * grp + h1, l0 : l0 + P, :].rearrange("h l d -> l h d"),
                in_=heads(rot, h0, h1),
            )

        def add_and_store(rot, cross, t, grp, h0, h1, adder=nc.vector):
            cols = slice(DH * h0, DH * h1)
            adder.tensor_tensor(out=rot[:, cols], in0=rot[:, cols], in1=cross[:, cols], op=ALU.add)
            store(rot, t, grp, h0, h1)

        def later_loads(u):
            if u == 0:
                load_x_planes(2)
                load_x_codes(2, 0, 4)
                load_x_codes(2, 4, PASSES)
            elif u == 2:
                load_w_planes(2, 0, PASSES)
            elif 3 <= u < 7:
                load_w_codes(2, 2 * (u - 3), 2 * (u - 2))

        units = [(t, grp) for grp in range(GROUPS) for t in range(TILES)]
        last = len(units) - 1

        warm = psum.tile([P, N_TILE], F32, name="bank%d" % (BANKS - 1))
        for i in range(WARM_MATMULS):
            nc.tensor.matmul(out=warm[:], lhsT=zeros[:, 0:P], rhs=zeros[:], start=True, stop=True)

        sweep = [(t, c) for t in range(SWEEP_TILES) for c in range(SWEEP_CHUNKS)]
        sweep_banks = {key: new_bank() for key in sweep}
        by_column = [(t, c) for c in range(SWEEP_CHUNKS) for t in range(SWEEP_TILES)]
        for g in range(PASSES):
            for t, c in by_column if g < PASSES - 1 else sweep:
                mm(sweep_banks[t, c], N_TILE, t, 0, N_TILE * c, g)
        sweep_proj = []
        for t in range(SWEEP_TILES):
            proj = work.tile([P, GF], F32, name="proj", bufs=PROJ_BUFS)
            for c in range(SWEEP_CHUNKS):
                nc.scalar.copy(out=proj[:, N_TILE * c : N_TILE * (c + 1)], in_=sweep_banks[t, c][:])
            sweep_proj.append(proj)

        whole = ((N_TILE, None), (N_TILE, None), (N_TILE, (0, GH)))
        by_chunk = ((N_TILE, (0, 2)), (N_TILE, (2, 5)), (N_TILE, (5, GH)))
        swept = ((N_TILE * SWEEP_CHUNKS, (0, SWEEP_HEADS)), (N_TILE, (SWEEP_HEADS, GH)))

        pending = None
        for u, (t, grp) in enumerate(units[:last]):
            if u < SWEEP_TILES:
                proj, spans = sweep_proj[u], swept
            else:
                proj = work.tile([P, GF], F32, name="proj", bufs=PROJ_BUFS)
                spans = by_chunk if u >= last - BY_CHUNK else whole
            cross = work.tile([P, GF], F32, name="cross", bufs=2)
            rot = work.tile([P, GF], F32, name="rot", bufs=3)
            c0 = 0
            for n, span in spans:
                if u >= SWEEP_TILES or c0 > 0:
                    bank = new_bank()
                    for g in range(PASSES):
                        mm(bank, n, t, grp, c0, g)
                    nc.scalar.copy(out=proj[:, c0 : c0 + n], in_=bank[:])
                c0 += n
                if span is None:
                    continue
                h0, h1 = span
                times_cos(proj, rot, t, h0, h1)
                if pending is not None:
                    add_and_store(*pending)
                times_sin(proj, cross, t, h0, h1)
                pending = (rot, cross, t, grp, h0, h1)
            if u in later_tables:
                make_tables(*later_tables[u])
            if u == TILES:
                make_wrapped_tables()
            later_loads(u - 1)
        add_and_store(*pending, adder=nc.gpsimd)

        t, grp = units[last]
        cross = work.tile([P, GF], F32, name="cross", bufs=2)
        rot = work.tile([P, GF], F32, name="rot", bufs=3)
        c0 = 0
        for i, (n, (h0, h1)) in enumerate(LAST_CHUNKS):
            bank = new_bank()
            for g in range(PASSES):
                mm(bank, n, t, grp, c0, g)
            cols = slice(c0, c0 + n)
            axis = c0 // D3 % AX
            table = slice(D3 * axis, D3 * axis + n)
            nc.vector.tensor_tensor(out=rot[:, cols], in0=bank[:, 0:n], in1=last_cos[:, table], op=ALU.mult)
            src = bank[:, 0:n].rearrange("p (m s i) -> p m s i", s=2, i=HALF)
            dst = cross[:, cols].rearrange("p (m s i) -> p m s i", s=2, i=HALF)
            sin = last_sin[:, table].rearrange("p (m s i) -> p m s i", s=2, i=HALF)
            for s in (0, 1):
                nc.vector.tensor_tensor(out=dst[:, :, s, :], in0=src[:, :, 1 - s, :], in1=sin[:, :, s, :], op=ALU.mult)
            adder = nc.gpsimd if i < GPSIMD_CHUNKS else nc.vector
            adder.tensor_tensor(out=rot[:, cols], in0=rot[:, cols], in1=cross[:, cols], op=ALU.add)
            store(rot, t, grp, h0, h1)
            c0 += n
